import numpy as np
import ml_dtypes


def mxq(x, axis, fmt="e4m3"):
    dtype, down = {"e4m3": (ml_dtypes.float8_e4m3fn, 7), "e5m2": (ml_dtypes.float8_e5m2, 14)}[fmt]
    v = np.moveaxis(np.asarray(x, np.float32).astype(ml_dtypes.bfloat16).astype(np.float64), axis, -1)
    blocks = v.reshape(v.shape[:-1] + (-1, 32))
    amax = np.abs(blocks).max(-1, keepdims=True)
    byte = np.maximum(np.where(amax > 0, np.frexp(amax)[1] - 1 + 127, 0) - down, 1)
    scale = np.exp2(byte - 127.0)
    codes = (blocks / scale).astype(np.float32).astype(dtype).astype(np.float64)
    return np.moveaxis((codes * scale).reshape(v.shape), -1, axis)


WIDE = False


def mx_kscale(k):
    if not WIDE:
        return np.ones(k)
    levels = np.array([10, -10, 5, -5, 0])
    a = np.random.permutation(np.resize(levels, k // 512 * 4)).reshape(k // 512, 4)
    idx = np.arange(k)
    return np.exp2(a[idx // 512, idx % 128 // 32])


BF16 = ml_dtypes.bfloat16


def bf(x):
    return np.asarray(x, np.float32).astype(BF16)


def f64(x):
    return np.asarray(x).astype(np.float64)


B, CK, CV, NO, T, H, W = 1, 128, 512, 3, 4, 16, 8
N = T * H * W
P = H * W
C = NO * CV


def setup_inputs():
    s = mx_kscale(N)
    g = np.exp2(np.round(np.log2(np.mean(s))))
    mk = np.random.standard_normal((B, CK, N))
    qk = np.random.standard_normal((B, CK, P))
    qe = np.random.uniform(0.0, 1.0, (B, CK, P))
    ms = bf(0.75 + 0.5 * np.random.uniform(0.0, 1.0, (B, N)))
    d = (np.log2(np.max(s)) - np.log2(s))[None, :] * np.log(2.0) * np.sqrt(CK) / f64(ms)
    a0 = mk[:, 0, :] ** 2 + d
    mk[:, 0, :] = np.sqrt(a0)
    qk[:, 0, :] = 0.0
    qe[:, 0, :] = 1.0
    mk, qk, qe = bf(mk), bf(qk), bf(qe)
    mksq = f64(mk) * f64(mk)
    mksq[:, 0, :] = a0
    return {"memory_key": mk,
            "memory_key_sq": bf(mksq),
            "query_key": qk,
            "query_selection": qe,
            "query_key_sel": bf(f64(qk) * f64(qe)),
            "memory_shrinkage": ms,
            "memory_value": bf(np.random.standard_normal((B, C, N)) * g / s[None, None, :])}


def reference(memory_key, memory_key_sq, query_key, query_selection, query_key_sel, memory_shrinkage, memory_value):
    qe = f64(query_selection)
    qs = f64(query_key_sel)
    ms = f64(memory_shrinkage)[:, :, None]
    a_sq = f64(memory_key_sq).transpose(0, 2, 1) @ qe
    two_ab = 2.0 * (f64(memory_key).transpose(0, 2, 1) @ qs)
    b_sq = np.sum(qs * f64(query_key), axis=1, keepdims=True)
    similarity = (-a_sq + two_ab - b_sq) * ms * (1.0 / np.sqrt(CK))
    e = np.exp(similarity - similarity.max(axis=1, keepdims=True))
    affinity = e / e.sum(axis=1, keepdims=True)
    return mxq(f64(memory_value), 2, "e4m3") @ mxq(affinity, 1, "e4m3")

@@ -1,0 +1,216 @@
+import math
+from contextlib import ExitStack
+
+import concourse.mybir as mybir
+from concourse.masks import make_identity
+
+F32 = mybir.dt.float32
+BF16 = mybir.dt.bfloat16
+U32 = mybir.dt.uint32
+U8 = mybir.dt.uint8
+FP8X4 = mybir.dt.float8_e4m3fn_x4
+ALU = mybir.AluOpType
+ACT = mybir.ActivationFunctionType
+AXIS = mybir.AxisListType
+
+PARTS = 128
+N_MEM = 512
+CHANNELS = 1536
+PACK = 4
+HALVES = 2
+PAIR = 2
+CH_TILES = CHANNELS // PARTS
+TILES_PER_LOAD = 4
+TILES_PER_BANK = 2
+
+FLOPS = 2 * CHANNELS * N_MEM * PARTS + 2 * (2 * N_MEM * PARTS * PARTS) + 2 * PARTS * PARTS
+
+
+def tile_vidsam_pa_s_kernel(
+    tc,
+    memory_key,
+    memory_key_sq,
+    query_key,
+    query_selection,
+    query_key_sel,
+    memory_shrinkage,
+    memory_value,
+    out,
+):
+    nc = tc.nc
+    with ExitStack() as ctx:
+        consts = ctx.enter_context(tc.tile_pool(name="consts", bufs=1))
+        inputs = ctx.enter_context(tc.tile_pool(name="inputs", bufs=1))
+        soft = ctx.enter_context(tc.tile_pool(name="soft", bufs=1))
+        quant = ctx.enter_context(tc.tile_pool(name="quant", bufs=1))
+        stream = ctx.enter_context(tc.tile_pool(name="stream", bufs=3))
+        psum_soft = ctx.enter_context(tc.psum_pool(name="psum_soft", bufs=1))
+        psum_banks = ctx.enter_context(tc.psum_pool(name="psum_banks", bufs=4))
+
+        qs_sb = inputs.tile([PARTS, PARTS], BF16)
+        nc.sync.dma_start(out=qs_sb[:], in_=query_key_sel[0])
+        mk_sb = inputs.tile([PARTS, N_MEM], BF16)
+        nc.sync.dma_start(out=mk_sb[:], in_=memory_key[0])
+        qe_sb = inputs.tile([PARTS, PARTS], BF16)
+        nc.sync.dma_start(out=qe_sb[:], in_=query_selection[0])
+        mksq_sb = inputs.tile([PARTS, N_MEM], BF16)
+        nc.sync.dma_start(out=mksq_sb[:], in_=memory_key_sq[0])
+        qk_sb = inputs.tile([PARTS, PARTS], BF16)
+        nc.sync.dma_start(out=qk_sb[:], in_=query_key[0])
+        ms_col = inputs.tile([PARTS, HALVES, PAIR], BF16)
+        with nc.allow_non_contiguous_dma(reason="512 values, in pieces of one pair"):
+            nc.sync.dma_start(
+                out=ms_col[:],
+                in_=memory_shrinkage[0].rearrange("(u q e) -> q u e", u=HALVES, e=PAIR),
+            )
+        mv_rows = memory_value[0].rearrange("(c j) n -> c j n", j=CH_TILES)
+        mv_loads = []
+        for first_tile in range(0, CH_TILES, TILES_PER_LOAD):
+            mv_sb = stream.tile([PARTS, TILES_PER_LOAD, N_MEM], BF16)
+            nc.sync.dma_start(
+                out=mv_sb[:], in_=mv_rows[:, first_tile : first_tile + TILES_PER_LOAD, :]
+            )
+            mv_loads.append(mv_sb)
+
+        ident_f32 = consts.tile([PARTS, PARTS], F32)
+        make_identity(nc, ident_f32[:])
+        ident_bf16 = consts.tile([PARTS, PARTS], BF16)
+        make_identity(nc, ident_bf16[:])
+        zero_col = consts.tile([PARTS, 1], F32)
+        nc.vector.memset(zero_col[:], 0.0)
+        one_col = consts.tile([PARTS, 1], F32)
+        nc.scalar.activation(out=one_col[:], in_=zero_col[:], func=ACT.Exp)
+
+        minus_two_qs = soft.tile([PARTS, PARTS], BF16)
+        nc.vector.tensor_scalar(
+            out=minus_two_qs[:], in0=qs_sb[:], scalar1=-2.0, scalar2=None, op0=ALU.mult
+        )
+        dist_ps = psum_soft.tile([PARTS, N_MEM], F32)
+        nc.tensor.matmul(dist_ps[:], lhsT=minus_two_qs[:], rhs=mk_sb[:], start=True, stop=False)
+        nc.tensor.matmul(dist_ps[:], lhsT=qe_sb[:], rhs=mksq_sb[:], start=False, stop=True)
+
+        gram_ps = psum_soft.tile([PARTS, PARTS], F32)
+        nc.tensor.matmul(gram_ps[:], lhsT=qs_sb[:], rhs=qk_sb[:], start=True, stop=True)
+        gram_diag = soft.tile([PARTS, PARTS], F32)
+        b_sq = soft.tile([PARTS, 1], F32)
+        nc.vector.scalar_tensor_tensor(
+            out=gram_diag[:],
+            in0=gram_ps[:],
+            scalar=1.0,
+            in1=ident_f32[:],
+            op0=ALU.mult,
+            op1=ALU.mult,
+            accum_out=b_sq[:],
+        )
+
+        ms_rows_ps = psum_soft.tile([PARTS, PAIR, HALVES, PARTS], BF16)
+        for u in range(HALVES):
+            for e in range(PAIR):
+                nc.tensor.transpose(
+                    ms_rows_ps[:, e, u, :],
+                    ms_col[:, u, e : e + 1].to_broadcast([PARTS, PARTS]),
+                    ident_bf16[:],
+                )
+        shrink = soft.tile([PARTS, PAIR, HALVES * PARTS], F32)
+        nc.scalar.mul(
+            out=shrink[:],
+            in_=ms_rows_ps[:].rearrange("p e u q -> p e (u q)"),
+            mul=1.0 / math.sqrt(PARTS),
+        )
+
+        neg_sim = soft.tile([PARTS, PAIR, HALVES * PARTS], F32)
+        nc.vector.scalar_tensor_tensor(
+            out=neg_sim[:],
+            in0=dist_ps[:].rearrange("p (w e) -> p e w", e=PAIR),
+            scalar=b_sq[:],
+            in1=shrink[:],
+            op0=ALU.add,
+            op1=ALU.mult,
+        )
+        neg_sim_flat = neg_sim[:].rearrange("p e w -> p (e w)")
+        neg_max = soft.tile([PARTS, 1], F32)
+        nc.vector.tensor_reduce(out=neg_max[:], in_=neg_sim_flat, axis=AXIS.X, op=ALU.min)
+        expo = soft.tile([PARTS, N_MEM], F32)
+        expo_sum = soft.tile([PARTS, 1], F32)
+        nc.scalar.activation(
+            out=expo[:],
+            in_=neg_sim_flat,
+            func=ACT.Exp,
+            bias=neg_max[:],
+            scale=-1.0,
+            accum_out=expo_sum[:],
+        )
+        inv_sum = soft.tile([PARTS, 1], F32)
+        nc.vector.reciprocal(out=inv_sum[:], in_=expo_sum[:])
+        affinity = soft.tile([PARTS, PAIR, HALVES, PARTS], BF16)
+        nc.vector.tensor_scalar(
+            out=affinity[:].rearrange("p e u q -> p (e u q)"),
+            in0=expo[:],
+            scalar1=inv_sum[:],
+            scalar2=None,
+            op0=ALU.mult,
+        )
+
+        mv_codes = quant.tile([PARTS, CHANNELS], U32, align_bytes=64)
+        mv_scales = quant.tile([PARTS, CHANNELS], U8, align_bytes=64)
+        for first_tile in range(0, CH_TILES, TILES_PER_BANK):
+            mv_sb = mv_loads[first_tile // TILES_PER_LOAD]
+            mv_words = mv_sb[:].bitcast(F32)
+            mv_t_ps = psum_banks.tile([PARTS, TILES_PER_BANK, HALVES, PARTS], F32, tag="bank")
+            for i in range(TILES_PER_BANK):
+                for u in range(HALVES):
+                    nc.tensor.transpose(
+                        mv_t_ps[:, i, u, :],
+                        mv_words[:, first_tile % TILES_PER_LOAD + i, u * PARTS : (u + 1) * PARTS],
+                        ident_f32[:],
+                    )
+            mv_grouped = stream.tile([PARTS, TILES_PER_BANK, PARTS, PACK], BF16, align_bytes=64)
+            nc.scalar.copy(
+                out=mv_grouped[:].bitcast(F32),
+                in_=mv_t_ps[:].rearrange("q i u c -> q i c u"),
+            )
+            bank_cols = slice(first_tile * PARTS, (first_tile + TILES_PER_BANK) * PARTS)
+            nc.vector.quantize_mx(
+                out=mv_codes[:, bank_cols].bitcast(FP8X4),
+                scales=mv_scales[:, bank_cols],
+                in_=mv_grouped[:].rearrange("q i c t -> q (i c t)"),
+            )
+
+        aff_t_ps = psum_soft.tile([PARTS, PACK, PARTS], BF16)
+        for u in range(HALVES):
+            for e in range(PAIR):
+                nc.tensor.transpose(
+                    aff_t_ps[:, PAIR * u + e, :], affinity[:, e, u, :], ident_bf16[:]
+                )
+        aff_grouped = soft.tile([PARTS, PARTS, PACK], BF16, align_bytes=64)
+        nc.vector.tensor_copy(out=aff_grouped[:], in_=aff_t_ps[:].rearrange("q t p -> q p t"))
+        aff_codes = quant.tile([PARTS, PARTS], U32, align_bytes=64)
+        aff_scales = quant.tile([PARTS, PARTS], U8, align_bytes=64)
+        nc.vector.quantize_mx(
+            out=aff_codes[:].bitcast(FP8X4),
+            scales=aff_scales[:],
+            in_=aff_grouped[:].rearrange("q p t -> q (p t)"),
+        )
+
+        out_rows = out[0].rearrange("(c j) p -> c j p", j=CH_TILES)
+        for store, first_tile in enumerate(range(0, CH_TILES, TILES_PER_LOAD)):
+            acc_ps = psum_banks.tile([PARTS, TILES_PER_LOAD, PARTS], F32, tag="bank")
+            for i in range(TILES_PER_LOAD):
+                tile_cols = slice((first_tile + i) * PARTS, (first_tile + i + 1) * PARTS)
+                nc.tensor.matmul_mx(
+                    out=acc_ps[:, i, :],
+                    lhsT=mv_codes[:, tile_cols].bitcast(FP8X4),
+                    lhsT_scale=mv_scales[:, tile_cols],
+                    rhs=aff_codes[:].bitcast(FP8X4),
+                    rhs_scale=aff_scales[:],
+                    start=True,
+                    stop=True,
+                )
+            result = stream.tile([PARTS, TILES_PER_LOAD, PARTS], F32)
+            if store % 2 == 0:
+                nc.vector.tensor_copy(out=result[:], in_=acc_ps[:])
+            else:
+                nc.scalar.copy(out=result[:], in_=acc_ps[:])
+            nc.sync.dma_start(
+                out=out_rows[:, first_tile : first_tile + TILES_PER_LOAD, :], in_=result[:]
+            )

@@ -22,6 +22,9 @@ PAIR = 2
 CH_TILES = CHANNELS // PARTS
 TILES_PER_LOAD = 4
 TILES_PER_BANK = 2
+MV_BANKS = CH_TILES // TILES_PER_BANK
+BANK_COLS = TILES_PER_BANK * PARTS
+PSUM_BANKS = 8
 
 FLOPS = 2 * CHANNELS * N_MEM * PARTS + 2 * (2 * N_MEM * PARTS * PARTS) + 2 * PARTS * PARTS
 
@@ -43,67 +46,75 @@ def tile_vidsam_pa_s_kernel(
         inputs = ctx.enter_context(tc.tile_pool(name="inputs", bufs=1))
         soft = ctx.enter_context(tc.tile_pool(name="soft", bufs=1))
         quant = ctx.enter_context(tc.tile_pool(name="quant", bufs=1))
-        stream = ctx.enter_context(tc.tile_pool(name="stream", bufs=3))
-        psum_soft = ctx.enter_context(tc.psum_pool(name="psum_soft", bufs=1))
-        psum_banks = ctx.enter_context(tc.psum_pool(name="psum_banks", bufs=4))
+        loads = ctx.enter_context(tc.tile_pool(name="loads", bufs=CH_TILES // TILES_PER_LOAD))
+        pieces = ctx.enter_context(tc.tile_pool(name="pieces", bufs=MV_BANKS))
+        banks = ctx.enter_context(tc.psum_pool(name="banks", bufs=PSUM_BANKS))
+        ctx.enter_context(tc.manual_schedule())
 
-        qs_sb = inputs.tile([PARTS, PARTS], BF16)
-        nc.sync.dma_start(out=qs_sb[:], in_=query_key_sel[0])
-        mk_sb = inputs.tile([PARTS, N_MEM], BF16)
-        nc.sync.dma_start(out=mk_sb[:], in_=memory_key[0])
+        ms_col = inputs.tile([PARTS, HALVES, PAIR], BF16)
+        with nc.allow_non_contiguous_dma(reason="512 values, in pieces of one pair"):
+            nc.scalar.dma_start(
+                out=ms_col[:],
+                in_=memory_shrinkage[0].rearrange("(u q e) -> q u e", u=HALVES, e=PAIR),
+            )
         qe_sb = inputs.tile([PARTS, PARTS], BF16)
         nc.sync.dma_start(out=qe_sb[:], in_=query_selection[0])
         mksq_sb = inputs.tile([PARTS, N_MEM], BF16)
         nc.sync.dma_start(out=mksq_sb[:], in_=memory_key_sq[0])
+        qs_sb = inputs.tile([PARTS, PARTS], BF16)
+        nc.sync.dma_start(out=qs_sb[:], in_=query_key_sel[0])
         qk_sb = inputs.tile([PARTS, PARTS], BF16)
         nc.sync.dma_start(out=qk_sb[:], in_=query_key[0])
-        ms_col = inputs.tile([PARTS, HALVES, PAIR], BF16)
-        with nc.allow_non_contiguous_dma(reason="512 values, in pieces of one pair"):
-            nc.sync.dma_start(
-                out=ms_col[:],
-                in_=memory_shrinkage[0].rearrange("(u q e) -> q u e", u=HALVES, e=PAIR),
-            )
+        mk_sb = inputs.tile([PARTS, N_MEM], BF16)
+        nc.sync.dma_start(out=mk_sb[:], in_=memory_key[0])
         mv_rows = memory_value[0].rearrange("(c j) n -> c j n", j=CH_TILES)
         mv_loads = []
         for first_tile in range(0, CH_TILES, TILES_PER_LOAD):
-            mv_sb = stream.tile([PARTS, TILES_PER_LOAD, N_MEM], BF16)
+            mv_sb = loads.tile([PARTS, TILES_PER_LOAD, N_MEM], BF16)
             nc.sync.dma_start(
                 out=mv_sb[:], in_=mv_rows[:, first_tile : first_tile + TILES_PER_LOAD, :]
             )
             mv_loads.append(mv_sb)
 
-        ident_f32 = consts.tile([PARTS, PARTS], F32)
-        make_identity(nc, ident_f32[:])
         ident_bf16 = consts.tile([PARTS, PARTS], BF16)
         make_identity(nc, ident_bf16[:])
+        ident_f32 = consts.tile([PARTS, PARTS], F32)
+        make_identity(nc, ident_f32[:])
         zero_col = consts.tile([PARTS, 1], F32)
         nc.vector.memset(zero_col[:], 0.0)
         one_col = consts.tile([PARTS, 1], F32)
         nc.scalar.activation(out=one_col[:], in_=zero_col[:], func=ACT.Exp)
 
-        minus_two_qs = soft.tile([PARTS, PARTS], BF16)
-        nc.vector.tensor_scalar(
-            out=minus_two_qs[:], in0=qs_sb[:], scalar1=-2.0, scalar2=None, op0=ALU.mult
-        )
-        dist_ps = psum_soft.tile([PARTS, N_MEM], F32)
-        nc.tensor.matmul(dist_ps[:], lhsT=minus_two_qs[:], rhs=mk_sb[:], start=True, stop=False)
-        nc.tensor.matmul(dist_ps[:], lhsT=qe_sb[:], rhs=mksq_sb[:], start=False, stop=True)
+        mv_codes = quant.tile([PARTS, CHANNELS], U32, align_bytes=64)
+        mv_scales = quant.tile([PARTS, CHANNELS], U8, align_bytes=64)
 
-        gram_ps = psum_soft.tile([PARTS, PARTS], F32)
-        nc.tensor.matmul(gram_ps[:], lhsT=qs_sb[:], rhs=qk_sb[:], start=True, stop=True)
-        gram_diag = soft.tile([PARTS, PARTS], F32)
-        b_sq = soft.tile([PARTS, 1], F32)
-        nc.vector.scalar_tensor_tensor(
-            out=gram_diag[:],
-            in0=gram_ps[:],
-            scalar=1.0,
-            in1=ident_f32[:],
-            op0=ALU.mult,
-            op1=ALU.mult,
-            accum_out=b_sq[:],
-        )
+        def transpose_and_regroup(piece):
+            first_tile = piece * TILES_PER_BANK
+            mv_words = mv_loads[first_tile // TILES_PER_LOAD][:].bitcast(F32)
+            mv_t_ps = banks.tile([PARTS, TILES_PER_BANK, HALVES, PARTS], F32, tag="bank")
+            for i in range(TILES_PER_BANK):
+                for u in range(HALVES):
+                    nc.tensor.transpose(
+                        mv_t_ps[:, i, u, :],
+                        mv_words[:, first_tile % TILES_PER_LOAD + i, u * PARTS : (u + 1) * PARTS],
+                        ident_f32[:],
+                    )
+            mv_grouped = pieces.tile([PARTS, TILES_PER_BANK, PARTS, PACK], BF16, align_bytes=64)
+            nc.scalar.copy(
+                out=mv_grouped[:].bitcast(F32),
+                in_=mv_t_ps[:].rearrange("q i u c -> q i c u"),
+            )
+            return mv_grouped
 
-        ms_rows_ps = psum_soft.tile([PARTS, PAIR, HALVES, PARTS], BF16)
+        def quantise(piece, mv_grouped):
+            piece_cols = slice(piece * BANK_COLS, (piece + 1) * BANK_COLS)
+            nc.vector.quantize_mx(
+                out=mv_codes[:, piece_cols].bitcast(FP8X4),
+                scales=mv_scales[:, piece_cols],
+                in_=mv_grouped[:].rearrange("q i c t -> q (i c t)"),
+            )
+
+        ms_rows_ps = banks.tile([PARTS, PAIR, HALVES, PARTS], BF16, tag="bank")
         for u in range(HALVES):
             for e in range(PAIR):
                 nc.tensor.transpose(
@@ -117,6 +128,29 @@ def tile_vidsam_pa_s_kernel(
             in_=ms_rows_ps[:].rearrange("p e u q -> p e (u q)"),
             mul=1.0 / math.sqrt(PARTS),
         )
+
+        dist_ps = banks.tile([PARTS, N_MEM], F32, tag="bank")
+        nc.tensor.matmul(dist_ps[:], lhsT=qe_sb[:], rhs=mksq_sb[:], start=True, stop=False)
+        gram_ps = banks.tile([PARTS, PARTS], F32, tag="bank")
+        nc.tensor.matmul(gram_ps[:], lhsT=qs_sb[:], rhs=qk_sb[:], start=True, stop=True)
+        minus_two_qs = soft.tile([PARTS, PARTS], BF16)
+        nc.vector.tensor_scalar(
+            out=minus_two_qs[:], in0=qs_sb[:], scalar1=-2.0, scalar2=None, op0=ALU.mult
+        )
+        nc.tensor.matmul(dist_ps[:], lhsT=minus_two_qs[:], rhs=mk_sb[:], start=False, stop=True)
+        gram_diag = soft.tile([PARTS, PARTS], F32)
+        b_sq = soft.tile([PARTS, 1], F32)
+        nc.vector.scalar_tensor_tensor(
+            out=gram_diag[:],
+            in0=gram_ps[:],
+            scalar=1.0,
+            in1=ident_f32[:],
+            op0=ALU.mult,
+            op1=ALU.mult,
+            accum_out=b_sq[:],
+        )
+
+        grouped = [transpose_and_regroup(0)]
 
         neg_sim = soft.tile([PARTS, PAIR, HALVES * PARTS], F32)
         nc.vector.scalar_tensor_tensor(
@@ -140,6 +174,7 @@ def tile_vidsam_pa_s_kernel(
             scale=-1.0,
             accum_out=expo_sum[:],
         )
+        quantise(0, grouped[0])
         inv_sum = soft.tile([PARTS, 1], F32)
         nc.vector.reciprocal(out=inv_sum[:], in_=expo_sum[:])
         affinity = soft.tile([PARTS, PAIR, HALVES, PARTS], BF16)
@@ -151,37 +186,18 @@ def tile_vidsam_pa_s_kernel(
             op0=ALU.mult,
         )
 
-        mv_codes = quant.tile([PARTS, CHANNELS], U32, align_bytes=64)
-        mv_scales = quant.tile([PARTS, CHANNELS], U8, align_bytes=64)
-        for first_tile in range(0, CH_TILES, TILES_PER_BANK):
-            mv_sb = mv_loads[first_tile // TILES_PER_LOAD]
-            mv_words = mv_sb[:].bitcast(F32)
-            mv_t_ps = psum_banks.tile([PARTS, TILES_PER_BANK, HALVES, PARTS], F32, tag="bank")
-            for i in range(TILES_PER_BANK):
-                for u in range(HALVES):
-                    nc.tensor.transpose(
-                        mv_t_ps[:, i, u, :],
-                        mv_words[:, first_tile % TILES_PER_LOAD + i, u * PARTS : (u + 1) * PARTS],
-                        ident_f32[:],
-                    )
-            mv_grouped = stream.tile([PARTS, TILES_PER_BANK, PARTS, PACK], BF16, align_bytes=64)
-            nc.scalar.copy(
-                out=mv_grouped[:].bitcast(F32),
-                in_=mv_t_ps[:].rearrange("q i u c -> q i c u"),
-            )
-            bank_cols = slice(first_tile * PARTS, (first_tile + TILES_PER_BANK) * PARTS)
-            nc.vector.quantize_mx(
-                out=mv_codes[:, bank_cols].bitcast(FP8X4),
-                scales=mv_scales[:, bank_cols],
-                in_=mv_grouped[:].rearrange("q i c t -> q (i c t)"),
-            )
+        for piece in range(1, MV_BANKS - 2):
+            grouped.append(transpose_and_regroup(piece))
+        quantise(1, grouped[1])
 
-        aff_t_ps = psum_soft.tile([PARTS, PACK, PARTS], BF16)
+        aff_t_ps = banks.tile([PARTS, PACK, PARTS], BF16, tag="bank")
         for u in range(HALVES):
             for e in range(PAIR):
                 nc.tensor.transpose(
                     aff_t_ps[:, PAIR * u + e, :], affinity[:, e, u, :], ident_bf16[:]
                 )
+        for piece in range(MV_BANKS - 2, MV_BANKS):
+            grouped.append(transpose_and_regroup(piece))
         aff_grouped = soft.tile([PARTS, PARTS, PACK], BF16, align_bytes=64)
         nc.vector.tensor_copy(out=aff_grouped[:], in_=aff_t_ps[:].rearrange("q t p -> q p t"))
         aff_codes = quant.tile([PARTS, PARTS], U32, align_bytes=64)
@@ -191,11 +207,14 @@ def tile_vidsam_pa_s_kernel(
             scales=aff_scales[:],
             in_=aff_grouped[:].rearrange("q p t -> q (p t)"),
         )
+        for piece in range(2, MV_BANKS):
+            quantise(piece, grouped[piece])
 
         out_rows = out[0].rearrange("(c j) p -> c j p", j=CH_TILES)
-        for store, first_tile in enumerate(range(0, CH_TILES, TILES_PER_LOAD)):
-            acc_ps = psum_banks.tile([PARTS, TILES_PER_LOAD, PARTS], F32, tag="bank")
-            for i in range(TILES_PER_LOAD):
+        for piece in range(MV_BANKS):
+            first_tile = piece * TILES_PER_BANK
+            acc_ps = banks.tile([PARTS, TILES_PER_BANK, PARTS], F32, tag="bank")
+            for i in range(TILES_PER_BANK):
                 tile_cols = slice((first_tile + i) * PARTS, (first_tile + i + 1) * PARTS)
                 nc.tensor.matmul_mx(
                     out=acc_ps[:, i, :],
@@ -206,11 +225,11 @@ def tile_vidsam_pa_s_kernel(
                     start=True,
                     stop=True,
                 )
-            result = stream.tile([PARTS, TILES_PER_LOAD, PARTS], F32)
-            if store % 2 == 0:
-                nc.vector.tensor_copy(out=result[:], in_=acc_ps[:])
-            else:
+            result = pieces.tile([PARTS, TILES_PER_BANK, PARTS], F32)
+            if piece % 2 == 0:
                 nc.scalar.copy(out=result[:], in_=acc_ps[:])
+            else:
+                nc.vector.tensor_copy(out=result[:], in_=acc_ps[:])
             nc.sync.dma_start(
-                out=out_rows[:, first_tile : first_tile + TILES_PER_LOAD, :], in_=result[:]
+                out=out_rows[:, first_tile : first_tile + TILES_PER_BANK, :], in_=result[:]
             )

@@ -25,6 +25,9 @@ TILES_PER_BANK = 2
 MV_BANKS = CH_TILES // TILES_PER_BANK
 BANK_COLS = TILES_PER_BANK * PARTS
 PSUM_BANKS = 8
+TRANSPOSED_BEFORE_AFFINITY = 5
+QUANTISED_BEFORE_AFFINITY = 3
+WARM_PASSES = 12
 
 FLOPS = 2 * CHANNELS * N_MEM * PARTS + 2 * (2 * N_MEM * PARTS * PARTS) + 2 * PARTS * PARTS
 
@@ -75,6 +78,25 @@ def tile_vidsam_pa_s_kernel(
                 out=mv_sb[:], in_=mv_rows[:, first_tile : first_tile + TILES_PER_LOAD, :]
             )
             mv_loads.append(mv_sb)
+
+        zeros = consts.tile([PARTS, PACK * PARTS], BF16, align_bytes=64)
+        nc.vector.memset(zeros[:], 0.0)
+        zero_codes = consts.tile([PARTS, PARTS], U32, align_bytes=64)
+        zero_scales = consts.tile([PARTS, PARTS], U8, align_bytes=64)
+        nc.vector.quantize_mx(
+            out=zero_codes[:].bitcast(FP8X4), scales=zero_scales[:], in_=zeros[:]
+        )
+        idle_ps = banks.tile([PARTS, PARTS], F32, tag="bank")
+        for k in range(WARM_PASSES):
+            nc.tensor.matmul_mx(
+                out=idle_ps[:],
+                lhsT=zero_codes[:].bitcast(FP8X4),
+                lhsT_scale=zero_scales[:],
+                rhs=zero_codes[:].bitcast(FP8X4),
+                rhs_scale=zero_scales[:],
+                start=True,
+                stop=True,
+            )
 
         ident_bf16 = consts.tile([PARTS, PARTS], BF16)
         make_identity(nc, ident_bf16[:])
@@ -186,9 +208,10 @@ def tile_vidsam_pa_s_kernel(
             op0=ALU.mult,
         )
 
-        for piece in range(1, MV_BANKS - 2):
+        for piece in range(1, TRANSPOSED_BEFORE_AFFINITY):
             grouped.append(transpose_and_regroup(piece))
-        quantise(1, grouped[1])
+        for piece in range(1, QUANTISED_BEFORE_AFFINITY):
+            quantise(piece, grouped[piece])
 
         aff_t_ps = banks.tile([PARTS, PACK, PARTS], BF16, tag="bank")
         for u in range(HALVES):
@@ -196,7 +219,7 @@ def tile_vidsam_pa_s_kernel(
                 nc.tensor.transpose(
                     aff_t_ps[:, PAIR * u + e, :], affinity[:, e, u, :], ident_bf16[:]
                 )
-        for piece in range(MV_BANKS - 2, MV_BANKS):
+        for piece in range(TRANSPOSED_BEFORE_AFFINITY, MV_BANKS):
             grouped.append(transpose_and_regroup(piece))
         aff_grouped = soft.tile([PARTS, PARTS, PACK], BF16, align_bytes=64)
         nc.vector.tensor_copy(out=aff_grouped[:], in_=aff_t_ps[:].rearrange("q t p -> q p t"))
@@ -207,7 +230,7 @@ def tile_vidsam_pa_s_kernel(
             scales=aff_scales[:],
             in_=aff_grouped[:].rearrange("q p t -> q (p t)"),
         )
-        for piece in range(2, MV_BANKS):
+        for piece in range(QUANTISED_BEFORE_AFFINITY, MV_BANKS):
             quantise(piece, grouped[piece])
 
         out_rows = out[0].rearrange("(c j) p -> c j p", j=CH_TILES)

@@ -27,7 +27,6 @@ BANK_COLS = TILES_PER_BANK * PARTS
 PSUM_BANKS = 8
 TRANSPOSED_BEFORE_AFFINITY = 5
 QUANTISED_BEFORE_AFFINITY = 3
-WARM_PASSES = 12
 
 FLOPS = 2 * CHANNELS * N_MEM * PARTS + 2 * (2 * N_MEM * PARTS * PARTS) + 2 * PARTS * PARTS
 
@@ -78,25 +77,6 @@ def tile_vidsam_pa_s_kernel(
                 out=mv_sb[:], in_=mv_rows[:, first_tile : first_tile + TILES_PER_LOAD, :]
             )
             mv_loads.append(mv_sb)
-
-        zeros = consts.tile([PARTS, PACK * PARTS], BF16, align_bytes=64)
-        nc.vector.memset(zeros[:], 0.0)
-        zero_codes = consts.tile([PARTS, PARTS], U32, align_bytes=64)
-        zero_scales = consts.tile([PARTS, PARTS], U8, align_bytes=64)
-        nc.vector.quantize_mx(
-            out=zero_codes[:].bitcast(FP8X4), scales=zero_scales[:], in_=zeros[:]
-        )
-        idle_ps = banks.tile([PARTS, PARTS], F32, tag="bank")
-        for k in range(WARM_PASSES):
-            nc.tensor.matmul_mx(
-                out=idle_ps[:],
-                lhsT=zero_codes[:].bitcast(FP8X4),
-                lhsT_scale=zero_scales[:],
-                rhs=zero_codes[:].bitcast(FP8X4),
-                rhs_scale=zero_scales[:],
-                start=True,
-                stop=True,
-            )
 
         ident_bf16 = consts.tile([PARTS, PARTS], BF16)
         make_identity(nc, ident_bf16[:])

import math
from contextlib import ExitStack

import concourse.mybir as mybir
from concourse.masks import make_identity

F32 = mybir.dt.float32
BF16 = mybir.dt.bfloat16
U32 = mybir.dt.uint32
U8 = mybir.dt.uint8
FP8X4 = mybir.dt.float8_e4m3fn_x4
ALU = mybir.AluOpType
ACT = mybir.ActivationFunctionType
AXIS = mybir.AxisListType

PARTS = 128
N_MEM = 512
CHANNELS = 1536
PACK = 4
HALVES = 2
PAIR = 2
CH_TILES = CHANNELS // PARTS
TILES_PER_LOAD = 4
TILES_PER_BANK = 2
MV_BANKS = CH_TILES // TILES_PER_BANK
BANK_COLS = TILES_PER_BANK * PARTS
PSUM_BANKS = 8
TRANSPOSED_BEFORE_AFFINITY = 5
QUANTISED_BEFORE_AFFINITY = 3

FLOPS = 2 * CHANNELS * N_MEM * PARTS + 2 * (2 * N_MEM * PARTS * PARTS) + 2 * PARTS * PARTS


def tile_vidsam_pa_s_kernel(
    tc,
    memory_key,
    memory_key_sq,
    query_key,
    query_selection,
    query_key_sel,
    memory_shrinkage,
    memory_value,
    out,
):
    nc = tc.nc
    with ExitStack() as ctx:
        consts = ctx.enter_context(tc.tile_pool(name="consts", bufs=1))
        inputs = ctx.enter_context(tc.tile_pool(name="inputs", bufs=1))
        soft = ctx.enter_context(tc.tile_pool(name="soft", bufs=1))
        quant = ctx.enter_context(tc.tile_pool(name="quant", bufs=1))
        loads = ctx.enter_context(tc.tile_pool(name="loads", bufs=CH_TILES // TILES_PER_LOAD))
        pieces = ctx.enter_context(tc.tile_pool(name="pieces", bufs=MV_BANKS))
        banks = ctx.enter_context(tc.psum_pool(name="banks", bufs=PSUM_BANKS))
        ctx.enter_context(tc.manual_schedule())

        ms_col = inputs.tile([PARTS, HALVES, PAIR], BF16)
        with nc.allow_non_contiguous_dma(reason="512 values, in pieces of one pair"):
            nc.scalar.dma_start(
                out=ms_col[:],
                in_=memory_shrinkage[0].rearrange("(u q e) -> q u e", u=HALVES, e=PAIR),
            )
        qe_sb = inputs.tile([PARTS, PARTS], BF16)
        nc.sync.dma_start(out=qe_sb[:], in_=query_selection[0])
        mksq_sb = inputs.tile([PARTS, N_MEM], BF16)
        nc.sync.dma_start(out=mksq_sb[:], in_=memory_key_sq[0])
        qs_sb = inputs.tile([PARTS, PARTS], BF16)
        nc.sync.dma_start(out=qs_sb[:], in_=query_key_sel[0])
        qk_sb = inputs.tile([PARTS, PARTS], BF16)
        nc.sync.dma_start(out=qk_sb[:], in_=query_key[0])
        mk_sb = inputs.tile([PARTS, N_MEM], BF16)
        nc.sync.dma_start(out=mk_sb[:], in_=memory_key[0])
        mv_rows = memory_value[0].rearrange("(c j) n -> c j n", j=CH_TILES)
        mv_loads = []
        for first_tile in range(0, CH_TILES, TILES_PER_LOAD):
            mv_sb = loads.tile([PARTS, TILES_PER_LOAD, N_MEM], BF16)
            nc.sync.dma_start(
                out=mv_sb[:], in_=mv_rows[:, first_tile : first_tile + TILES_PER_LOAD, :]
            )
            mv_loads.append(mv_sb)

        ident_bf16 = consts.tile([PARTS, PARTS], BF16)
        make_identity(nc, ident_bf16[:])
        ident_f32 = consts.tile([PARTS, PARTS], F32)
        make_identity(nc, ident_f32[:])
        zero_col = consts.tile([PARTS, 1], F32)
        nc.vector.memset(zero_col[:], 0.0)
        one_col = consts.tile([PARTS, 1], F32)
        nc.scalar.activation(out=one_col[:], in_=zero_col[:], func=ACT.Exp)

        mv_codes = quant.tile([PARTS, CHANNELS], U32, align_bytes=64)
        mv_scales = quant.tile([PARTS, CHANNELS], U8, align_bytes=64)

        def transpose_and_regroup(piece):
            first_tile = piece * TILES_PER_BANK
            mv_words = mv_loads[first_tile // TILES_PER_LOAD][:].bitcast(F32)
            mv_t_ps = banks.tile([PARTS, TILES_PER_BANK, HALVES, PARTS], F32, tag="bank")
            for i in range(TILES_PER_BANK):
                for u in range(HALVES):
                    nc.tensor.transpose(
                        mv_t_ps[:, i, u, :],
                        mv_words[:, first_tile % TILES_PER_LOAD + i, u * PARTS : (u + 1) * PARTS],
                        ident_f32[:],
                    )
            mv_grouped = pieces.tile([PARTS, TILES_PER_BANK, PARTS, PACK], BF16, align_bytes=64)
            nc.scalar.copy(
                out=mv_grouped[:].bitcast(F32),
                in_=mv_t_ps[:].rearrange("q i u c -> q i c u"),
            )
            return mv_grouped

        def quantise(piece, mv_grouped):
            piece_cols = slice(piece * BANK_COLS, (piece + 1) * BANK_COLS)
            nc.vector.quantize_mx(
                out=mv_codes[:, piece_cols].bitcast(FP8X4),
                scales=mv_scales[:, piece_cols],
                in_=mv_grouped[:].rearrange("q i c t -> q (i c t)"),
            )

        ms_rows_ps = banks.tile([PARTS, PAIR, HALVES, PARTS], BF16, tag="bank")
        for u in range(HALVES):
            for e in range(PAIR):
                nc.tensor.transpose(
                    ms_rows_ps[:, e, u, :],
                    ms_col[:, u, e : e + 1].to_broadcast([PARTS, PARTS]),
                    ident_bf16[:],
                )
        shrink = soft.tile([PARTS, PAIR, HALVES * PARTS], F32)
        nc.scalar.mul(
            out=shrink[:],
            in_=ms_rows_ps[:].rearrange("p e u q -> p e (u q)"),
            mul=1.0 / math.sqrt(PARTS),
        )

        dist_ps = banks.tile([PARTS, N_MEM], F32, tag="bank")
        nc.tensor.matmul(dist_ps[:], lhsT=qe_sb[:], rhs=mksq_sb[:], start=True, stop=False)
        gram_ps = banks.tile([PARTS, PARTS], F32, tag="bank")
        nc.tensor.matmul(gram_ps[:], lhsT=qs_sb[:], rhs=qk_sb[:], start=True, stop=True)
        minus_two_qs = soft.tile([PARTS, PARTS], BF16)
        nc.vector.tensor_scalar(
            out=minus_two_qs[:], in0=qs_sb[:], scalar1=-2.0, scalar2=None, op0=ALU.mult
        )
        nc.tensor.matmul(dist_ps[:], lhsT=minus_two_qs[:], rhs=mk_sb[:], start=False, stop=True)
        gram_diag = soft.tile([PARTS, PARTS], F32)
        b_sq = soft.tile([PARTS, 1], F32)
        nc.vector.scalar_tensor_tensor(
            out=gram_diag[:],
            in0=gram_ps[:],
            scalar=1.0,
            in1=ident_f32[:],
            op0=ALU.mult,
            op1=ALU.mult,
            accum_out=b_sq[:],
        )

        grouped = [transpose_and_regroup(0)]

        neg_sim = soft.tile([PARTS, PAIR, HALVES * PARTS], F32)
        nc.vector.scalar_tensor_tensor(
            out=neg_sim[:],
            in0=dist_ps[:].rearrange("p (w e) -> p e w", e=PAIR),
            scalar=b_sq[:],
            in1=shrink[:],
            op0=ALU.add,
            op1=ALU.mult,
        )
        neg_sim_flat = neg_sim[:].rearrange("p e w -> p (e w)")
        neg_max = soft.tile([PARTS, 1], F32)
        nc.vector.tensor_reduce(out=neg_max[:], in_=neg_sim_flat, axis=AXIS.X, op=ALU.min)
        expo = soft.tile([PARTS, N_MEM], F32)
        expo_sum = soft.tile([PARTS, 1], F32)
        nc.scalar.activation(
            out=expo[:],
            in_=neg_sim_flat,
            func=ACT.Exp,
            bias=neg_max[:],
            scale=-1.0,
            accum_out=expo_sum[:],
        )
        quantise(0, grouped[0])
        inv_sum = soft.tile([PARTS, 1], F32)
        nc.vector.reciprocal(out=inv_sum[:], in_=expo_sum[:])
        affinity = soft.tile([PARTS, PAIR, HALVES, PARTS], BF16)
        nc.vector.tensor_scalar(
            out=affinity[:].rearrange("p e u q -> p (e u q)"),
            in0=expo[:],
            scalar1=inv_sum[:],
            scalar2=None,
            op0=ALU.mult,
        )

        for piece in range(1, TRANSPOSED_BEFORE_AFFINITY):
            grouped.append(transpose_and_regroup(piece))
        for piece in range(1, QUANTISED_BEFORE_AFFINITY):
            quantise(piece, grouped[piece])

        aff_t_ps = banks.tile([PARTS, PACK, PARTS], BF16, tag="bank")
        for u in range(HALVES):
            for e in range(PAIR):
                nc.tensor.transpose(
                    aff_t_ps[:, PAIR * u + e, :], affinity[:, e, u, :], ident_bf16[:]
                )
        for piece in range(TRANSPOSED_BEFORE_AFFINITY, MV_BANKS):
            grouped.append(transpose_and_regroup(piece))
        aff_grouped = soft.tile([PARTS, PARTS, PACK], BF16, align_bytes=64)
        nc.vector.tensor_copy(out=aff_grouped[:], in_=aff_t_ps[:].rearrange("q t p -> q p t"))
        aff_codes = quant.tile([PARTS, PARTS], U32, align_bytes=64)
        aff_scales = quant.tile([PARTS, PARTS], U8, align_bytes=64)
        nc.vector.quantize_mx(
            out=aff_codes[:].bitcast(FP8X4),
            scales=aff_scales[:],
            in_=aff_grouped[:].rearrange("q p t -> q (p t)"),
        )
        for piece in range(QUANTISED_BEFORE_AFFINITY, MV_BANKS):
            quantise(piece, grouped[piece])

        out_rows = out[0].rearrange("(c j) p -> c j p", j=CH_TILES)
        for piece in range(MV_BANKS):
            first_tile = piece * TILES_PER_BANK
            acc_ps = banks.tile([PARTS, TILES_PER_BANK, PARTS], F32, tag="bank")
            for i in range(TILES_PER_BANK):
                tile_cols = slice((first_tile + i) * PARTS, (first_tile + i + 1) * PARTS)
                nc.tensor.matmul_mx(
                    out=acc_ps[:, i, :],
                    lhsT=mv_codes[:, tile_cols].bitcast(FP8X4),
                    lhsT_scale=mv_scales[:, tile_cols],
                    rhs=aff_codes[:].bitcast(FP8X4),
                    rhs_scale=aff_scales[:],
                    start=True,
                    stop=True,
                )
            result = pieces.tile([PARTS, TILES_PER_BANK, PARTS], F32)
            if piece % 2 == 0:
                nc.scalar.copy(out=result[:], in_=acc_ps[:])
            else:
                nc.vector.tensor_copy(out=result[:], in_=acc_ps[:])
            nc.sync.dma_start(
                out=out_rows[:, first_tile : first_tile + TILES_PER_BANK, :], in_=result[:]
            )
